import numpy as np
import ml_dtypes


def mxq(x, axis, fmt="e4m3"):
    dtype, down = {"e4m3": (ml_dtypes.float8_e4m3fn, 7), "e5m2": (ml_dtypes.float8_e5m2, 14)}[fmt]
    v = np.moveaxis(np.asarray(x, np.float32).astype(ml_dtypes.bfloat16).astype(np.float64), axis, -1)
    blocks = v.reshape(v.shape[:-1] + (-1, 32))
    amax = np.abs(blocks).max(-1, keepdims=True)
    byte = np.maximum(np.where(amax > 0, np.frexp(amax)[1] - 1 + 127, 0) - down, 1)
    scale = np.exp2(byte - 127.0)
    codes = (blocks / scale).astype(np.float32).astype(dtype).astype(np.float64)
    return np.moveaxis((codes * scale).reshape(v.shape), -1, axis)


WIDE = False


def mx_kscale(k):
    if not WIDE:
        return np.ones(k)
    levels = np.array([20, -20, 10, -10, 0])
    a = np.random.permutation(np.resize(levels, k // 512 * 4)).reshape(k // 512, 4)
    idx = np.arange(k)
    return np.exp2(a[idx // 512, idx % 128 // 32])


BF16 = ml_dtypes.bfloat16


def bf(x):
    return np.asarray(x, np.float32).astype(BF16)


def f64(x):
    return np.asarray(x).astype(np.float64)


B, IN, OUT, G = 1024, 512, 512, 20


def silu(v):
    with np.errstate(over="ignore"):
        return v / (1.0 + np.exp(-v))


def setup_inputs():
    bound = 1.0 / np.sqrt(IN)
    s = mx_kscale(B)
    c = np.maximum(s, 1.0)[:, None]
    x = np.random.standard_normal((B, IN)) * c
    base_weight = np.random.uniform(-bound, bound, (OUT, IN))
    spline_weight = 0.05 * np.random.standard_normal((OUT, IN, G))
    spline_scale = 0.1 * (1.0 + 0.1 * np.random.standard_normal((OUT, 1, 1)))
    grid = np.linspace(-2.0, 2.0, G)
    g = np.random.standard_normal((B, OUT)) * np.exp2(np.random.randint(-12, 1, (B, 1))) * 4.0 / c
    return {"x": bf(x), "base_weight": bf(base_weight), "spline_weight": bf(spline_weight),
            "spline_scale": bf(spline_scale), "grid": bf(grid), "grad_out": bf(g)}


def reference(x, base_weight, spline_weight, spline_scale, grid, grad_out):
    x, spline_scale, grid, grad_out = f64(x), f64(spline_scale), f64(grid), f64(grad_out)
    basis = np.maximum(x[:, :, None] - grid[None, None, :], 0.0)
    basis_f = basis.reshape(basis.shape[0], -1)
    p = mxq(grad_out, 0, "e5m2").T @ mxq(basis_f, 0, "e4m3")
    return p.reshape(grad_out.shape[1], x.shape[1], grid.shape[0]) * spline_scale

@@ -1,0 +1,212 @@
+from contextlib import ExitStack
+
+import concourse.mybir as mybir
+
+F32 = mybir.dt.float32
+BF16 = mybir.dt.bfloat16
+U32 = mybir.dt.uint32
+U8 = mybir.dt.uint8
+E4X4 = mybir.dt.float8_e4m3fn_x4
+E5X4 = mybir.dt.float8_e5m2_x4
+ALU = mybir.AluOpType
+ACT = mybir.ActivationFunctionType
+
+B, IN, OUT, G = 1024, 512, 512, 20
+P = 128
+PACK = 4
+PASSES = B // (P * PACK)
+MT = OUT // P
+NCOL = 512
+NT = IN * G // NCOL
+
+FLOPS = 2 * B * OUT * IN * G
+BYTES = 2 * B * IN + 2 * B * OUT + 2 * OUT + 2 * G + 4 * OUT * IN * G
+
+UNITS = [64] * 8
+MANUAL = True
+S_XRG_AFTER = {3: 2, 8: 3}
+OSB_BUFS = 16
+
+
+def tile_relukanlayer_kernel(tc, x, base_weight, spline_weight, spline_scale, grid, grad_out, out):
+    nc = tc.nc
+
+    units = []
+    i0 = 0
+    for r in UNITS:
+        units.append((i0, r))
+        i0 += r
+    assert i0 == IN
+    tile_rows = []
+    tile_segs = []
+    for n in range(NT):
+        tile_rows.append([])
+        tile_segs.append([])
+    last_tile = []
+    for u in range(len(units)):
+        i0, r = units[u]
+        for g in range(G):
+            col = G * i0 + g * r
+            n = col // NCOL
+            tile_rows[n].append((u, g, col % NCOL))
+            segs = tile_segs[n]
+            if len(segs) > 0 and segs[-1][0] == u:
+                segs[-1] = (u, segs[-1][1], segs[-1][2] + 1, segs[-1][3])
+            else:
+                segs.append((u, g, 1, col % NCOL))
+        last_tile.append(n)
+
+    with ExitStack() as ctx:
+        keep = ctx.enter_context(tc.tile_pool(name="keep", bufs=1))
+        work = ctx.enter_context(tc.tile_pool(name="work", bufs=3))
+        outp = ctx.enter_context(tc.tile_pool(name="outp", bufs=OSB_BUFS))
+        psum = ctx.enter_context(tc.psum_pool(name="psum", bufs=8))
+        if MANUAL:
+            ctx.enter_context(tc.manual_schedule())
+
+        xa_raw = []
+        xr_raw = []
+        g_raw = []
+        gg = []
+        g_codes = []
+        g_scales = []
+        for c in range(PASSES):
+            xa_raw.append(keep.tile([P, PACK, P], BF16, name="xa_raw%d" % c))
+            xr_raw.append(keep.tile([P, PACK, IN - P], BF16, name="xr_raw%d" % c))
+            g_raw.append(keep.tile([P, PACK, OUT], BF16, name="g_raw%d" % c))
+            gg.append(keep.tile([P, PACK * OUT], BF16, name="gg%d" % c, align_bytes=64))
+            g_codes.append(keep.tile([P, OUT], U32, name="g_codes%d" % c, align_bytes=64))
+            g_scales.append(keep.tile([P, OUT], U8, name="g_scales%d" % c, align_bytes=64))
+        xg = []
+        for blk in range(IN // P):
+            xg.append(keep.tile([P, PASSES, PACK * P], BF16, name="xg%d" % blk))
+        grid_b = keep.tile([P, G], BF16, name="grid_b")
+        grid_f = keep.tile([P, G], F32, name="grid_f")
+        sc_b = keep.tile([P, MT], BF16, name="sc_b")
+        sc_f = keep.tile([P, MT], F32, name="sc_f")
+
+        x_v = x.rearrange("(c p j) i -> p c j i", c=PASSES, p=P, j=PACK)
+        g_v = grad_out.rearrange("(c p j) o -> p c j o", c=PASSES, p=P, j=PACK)
+
+        nc.sync.dma_start(out=grid_b[:], in_=grid.partition_broadcast(P))
+        for c in range(PASSES):
+            nc.sync.dma_start(out=xa_raw[c][:], in_=x_v[:, c, :, 0:P])
+        for c in range(PASSES):
+            nc.scalar.dma_start(out=g_raw[c][:], in_=g_v[:, c, :, :])
+        with nc.allow_non_contiguous_dma(reason="512 scales, one to a partition and m-tile"):
+            nc.sync.dma_start(out=sc_b[:], in_=spline_scale.rearrange("(m p) a b -> p (m a b)", p=P))
+        for c in range(PASSES):
+            nc.scalar.dma_start(out=xr_raw[c][:], in_=x_v[:, c, :, P:IN])
+
+        nc.vector.tensor_copy(out=grid_f[:], in_=grid_b[:])
+        nc.gpsimd.tensor_copy(out=sc_f[:], in_=sc_b[:])
+
+        def regroup(eng, dst, src):
+            d = dst.rearrange("p (q r j) -> p q j r", r=4, j=PACK)
+            s = src.rearrange("p j (q r) -> p q j r", r=4)
+            if eng == "V":
+                nc.vector.tensor_copy(out=d, in_=s)
+            else:
+                nc.scalar.copy(out=d, in_=s)
+
+        def x_regroup(eng, blk):
+            for c in range(PASSES):
+                if blk == 0:
+                    regroup(eng, xg[blk][:, c, :], xa_raw[c][:])
+                else:
+                    regroup(eng, xg[blk][:, c, :], xr_raw[c][:, :, P * (blk - 1) : P * blk])
+
+        def g_regroup(eng, c):
+            regroup(eng, gg[c][:], g_raw[c][:])
+
+        def g_quant(c):
+            nc.vector.quantize_mx(out=g_codes[c][:].bitcast(E5X4), scales=g_scales[c][:], in_=gg[c][:])
+
+        bt = {}
+        bc = {}
+        bs = {}
+        acc = {}
+        osb = {}
+
+        def basis(n):
+            t = work.tile([P, PASSES, PACK * NCOL], BF16, name="bt%d" % n, tag="bt", align_bytes=64)
+            bt[n] = t
+            for u, g, col in tile_rows[n]:
+                i0, r = units[u]
+                nc.vector.tensor_scalar(
+                    out=t[:, :, PACK * col : PACK * (col + r)],
+                    in0=xg[i0 // P][:, :, PACK * (i0 % P) : PACK * (i0 % P + r)],
+                    scalar1=grid_f[:, g : g + 1],
+                    scalar2=0.0,
+                    op0=ALU.subtract,
+                    op1=ALU.max,
+                )
+
+        def quant(n):
+            codes = work.tile([P, PASSES, NCOL], U32, name="bc%d" % n, tag="bc", align_bytes=64)
+            scales = work.tile([P, PASSES, NCOL], U8, name="bs%d" % n, tag="bs", align_bytes=64)
+            bc[n] = codes
+            bs[n] = scales
+            nc.vector.quantize_mx(
+                out=codes[:].rearrange("p c w -> p (c w)").bitcast(E4X4),
+                scales=scales[:].rearrange("p c w -> p (c w)"),
+                in_=bt[n][:].rearrange("p c w -> p (c w)"),
+            )
+
+        def one_pass(n, m, c):
+            nc.tensor.matmul_mx(
+                out=acc[(n, m)][:],
+                lhsT=g_codes[c][:, P * m : P * (m + 1)].bitcast(E5X4),
+                lhsT_scale=g_scales[c][:, P * m : P * (m + 1)],
+                rhs=bc[n][:, c, :].bitcast(E4X4),
+                rhs_scale=bs[n][:, c, :],
+                start=(c == 0),
+                stop=(c == PASSES - 1),
+            )
+
+        def mm(n, c_major):
+            for m in range(MT):
+                acc[(n, m)] = psum.tile([P, NCOL], F32, name="acc%d_%d" % (n, m), tag="acc")
+            if c_major:
+                for c in range(PASSES):
+                    for m in range(MT):
+                        one_pass(n, m, c)
+            else:
+                for m in range(MT):
+                    for c in range(PASSES):
+                        one_pass(n, m, c)
+
+        def evac(n):
+            for m in range(MT):
+                for u, g0, gn, col in tile_segs[n]:
+                    i0, r = units[u]
+                    if (u, m) not in osb:
+                        osb[(u, m)] = outp.tile([P, r, G], F32, name="osb%d_%d" % (u, m), tag="osb")
+                    nc.scalar.activation(
+                        out=osb[(u, m)][:, :, g0 : g0 + gn],
+                        in_=acc[(n, m)][:, col : col + gn * r].rearrange("p (g i) -> p i g", g=gn),
+                        func=ACT.Copy,
+                        scale=sc_f[:, m : m + 1],
+                    )
+                    if last_tile[u] == n:
+                        nc.sync.dma_start(out=out[P * m : P * (m + 1), i0 : i0 + r, :], in_=osb[(u, m)][:])
+
+        x_regroup("V", 0)
+        g_regroup("S", 0)
+        g_regroup("S", 1)
+        x_regroup("S", 1)
+        basis(0)
+        quant(0)
+        g_quant(0)
+        basis(1)
+        g_quant(1)
+        mm(0, True)
+        evac(0)
+        for s in range(1, NT):
+            if s + 1 < NT:
+                basis(s + 1)
+            quant(s)
+            mm(s, False)
+            evac(s)
+            if s in S_XRG_AFTER:
+                x_regroup("S", S_XRG_AFTER[s])

@@ -24,7 +24,8 @@ BYTES = 2 * B * IN + 2 * B * OUT + 2 * OUT + 2 * G + 4 * OUT * IN * G
 
 UNITS = [64] * 8
 MANUAL = True
-S_XRG_AFTER = {3: 2, 8: 3}
+S_XRG_AFTER = {}
+V_XRG_BEFORE = {8: 2, 13: 3}
 OSB_BUFS = 16
 
 
@@ -92,11 +93,11 @@ def tile_relukanlayer_kernel(tc, x, base_weight, spline_weight, spline_scale, gr
         for c in range(PASSES):
             nc.sync.dma_start(out=xa_raw[c][:], in_=x_v[:, c, :, 0:P])
         for c in range(PASSES):
-            nc.scalar.dma_start(out=g_raw[c][:], in_=g_v[:, c, :, :])
+            nc.sync.dma_start(out=g_raw[c][:], in_=g_v[:, c, :, :])
         with nc.allow_non_contiguous_dma(reason="512 scales, one to a partition and m-tile"):
             nc.sync.dma_start(out=sc_b[:], in_=spline_scale.rearrange("(m p) a b -> p (m a b)", p=P))
         for c in range(PASSES):
-            nc.scalar.dma_start(out=xr_raw[c][:], in_=x_v[:, c, :, P:IN])
+            nc.sync.dma_start(out=xr_raw[c][:], in_=x_v[:, c, :, P:IN])
 
         nc.vector.tensor_copy(out=grid_f[:], in_=grid_b[:])
         nc.gpsimd.tensor_copy(out=sc_f[:], in_=sc_b[:])
@@ -203,6 +204,8 @@ def tile_relukanlayer_kernel(tc, x, base_weight, spline_weight, spline_scale, gr
         mm(0, True)
         evac(0)
         for s in range(1, NT):
+            if s in V_XRG_BEFORE:
+                x_regroup("V", V_XRG_BEFORE[s])
             if s + 1 < NT:
                 basis(s + 1)
             quant(s)

@@ -23,10 +23,13 @@ FLOPS = 2 * B * OUT * IN * G
 BYTES = 2 * B * IN + 2 * B * OUT + 2 * OUT + 2 * G + 4 * OUT * IN * G
 
 UNITS = [64] * 8
-MANUAL = True
-S_XRG_AFTER = {}
-V_XRG_BEFORE = {8: 2, 13: 3}
+PIECES = [(0, 64), (64, 64), (128, 128), (256, 128), (384, 128)]
+S_XRG_AFTER = {3: 3, 8: 4}
+V_XRG_BEFORE = {}
+V_EVAC_M = ()
 OSB_BUFS = 16
+LEAD_ELEMS = 1280
+G1_SPLIT = True
 
 
 def tile_relukanlayer_kernel(tc, x, base_weight, spline_weight, spline_scale, grid, grad_out, out):
@@ -56,14 +59,14 @@ def tile_relukanlayer_kernel(tc, x, base_weight, spline_weight, spline_scale, gr
             else:
                 segs.append((u, g, 1, col % NCOL))
         last_tile.append(n)
+    last_unit = len(units) - 1
 
     with ExitStack() as ctx:
         keep = ctx.enter_context(tc.tile_pool(name="keep", bufs=1))
         work = ctx.enter_context(tc.tile_pool(name="work", bufs=3))
         outp = ctx.enter_context(tc.tile_pool(name="outp", bufs=OSB_BUFS))
         psum = ctx.enter_context(tc.psum_pool(name="psum", bufs=8))
-        if MANUAL:
-            ctx.enter_context(tc.manual_schedule())
+        ctx.enter_context(tc.manual_schedule())
 
         xa_raw = []
         xr_raw = []
@@ -79,8 +82,8 @@ def tile_relukanlayer_kernel(tc, x, base_weight, spline_weight, spline_scale, gr
             g_codes.append(keep.tile([P, OUT], U32, name="g_codes%d" % c, align_bytes=64))
             g_scales.append(keep.tile([P, OUT], U8, name="g_scales%d" % c, align_bytes=64))
         xg = []
-        for blk in range(IN // P):
-            xg.append(keep.tile([P, PASSES, PACK * P], BF16, name="xg%d" % blk))
+        for k in range(len(PIECES)):
+            xg.append(keep.tile([P, PASSES, PACK * PIECES[k][1]], BF16, name="xg%d" % k))
         grid_b = keep.tile([P, G], BF16, name="grid_b")
         grid_f = keep.tile([P, G], F32, name="grid_f")
         sc_b = keep.tile([P, MT], BF16, name="sc_b")
@@ -110,18 +113,25 @@ def tile_relukanlayer_kernel(tc, x, base_weight, spline_weight, spline_scale, gr
             else:
                 nc.scalar.copy(out=d, in_=s)
 
-        def x_regroup(eng, blk):
+        def x_regroup(eng, k):
+            a, w = PIECES[k]
             for c in range(PASSES):
-                if blk == 0:
-                    regroup(eng, xg[blk][:, c, :], xa_raw[c][:])
+                if a < P:
+                    regroup(eng, xg[k][:, c, :], xa_raw[c][:, :, a : a + w])
                 else:
-                    regroup(eng, xg[blk][:, c, :], xr_raw[c][:, :, P * (blk - 1) : P * blk])
+                    regroup(eng, xg[k][:, c, :], xr_raw[c][:, :, a - P : a - P + w])
 
-        def g_regroup(eng, c):
-            regroup(eng, gg[c][:], g_raw[c][:])
+        def g_regroup(eng, c, lo, hi):
+            regroup(eng, gg[c][:, PACK * lo : PACK * hi], g_raw[c][:, :, lo:hi])
 
         def g_quant(c):
             nc.vector.quantize_mx(out=g_codes[c][:].bitcast(E5X4), scales=g_scales[c][:], in_=gg[c][:])
+
+        def piece_of(i0):
+            for k in range(len(PIECES)):
+                if PIECES[k][0] <= i0 < PIECES[k][0] + PIECES[k][1]:
+                    return k
+            return -1
 
         bt = {}
         bc = {}
@@ -129,30 +139,52 @@ def tile_relukanlayer_kernel(tc, x, base_weight, spline_weight, spline_scale, gr
         acc = {}
         osb = {}
 
-        def basis(n):
-            t = work.tile([P, PASSES, PACK * NCOL], BF16, name="bt%d" % n, tag="bt", align_bytes=64)
-            bt[n] = t
+        def lead_rows(n):
+            k = 0
+            elems = 0
             for u, g, col in tile_rows[n]:
+                if elems < LEAD_ELEMS:
+                    elems += PASSES * PACK * units[u][1]
+                    k += 1
+            return k
+
+        def basis(n, part):
+            if n not in bt:
+                bt[n] = work.tile([P, PASSES, PACK * NCOL], BF16, name="bt%d" % n, tag="bt", align_bytes=64)
+            t = bt[n]
+            k = lead_rows(n)
+            rows = tile_rows[n]
+            if part == "a":
+                rows = tile_rows[n][:k]
+            if part == "b":
+                rows = tile_rows[n][k:]
+            for u, g, col in rows:
                 i0, r = units[u]
+                k = piece_of(i0)
+                off = i0 - PIECES[k][0]
                 nc.vector.tensor_scalar(
                     out=t[:, :, PACK * col : PACK * (col + r)],
-                    in0=xg[i0 // P][:, :, PACK * (i0 % P) : PACK * (i0 % P + r)],
+                    in0=xg[k][:, :, PACK * off : PACK * (off + r)],
                     scalar1=grid_f[:, g : g + 1],
                     scalar2=0.0,
                     op0=ALU.subtract,
                     op1=ALU.max,
                 )
 
-        def quant(n):
+        def quant(n, split):
             codes = work.tile([P, PASSES, NCOL], U32, name="bc%d" % n, tag="bc", align_bytes=64)
             scales = work.tile([P, PASSES, NCOL], U8, name="bs%d" % n, tag="bs", align_bytes=64)
             bc[n] = codes
             bs[n] = scales
-            nc.vector.quantize_mx(
-                out=codes[:].rearrange("p c w -> p (c w)").bitcast(E4X4),
-                scales=scales[:].rearrange("p c w -> p (c w)"),
-                in_=bt[n][:].rearrange("p c w -> p (c w)"),
-            )
+            if split:
+                for c in range(PASSES):
+                    nc.vector.quantize_mx(out=codes[:, c, :].bitcast(E4X4), scales=scales[:, c, :], in_=bt[n][:, c, :])
+            else:
+                nc.vector.quantize_mx(
+                    out=codes[:].rearrange("p c w -> p (c w)").bitcast(E4X4),
+                    scales=scales[:].rearrange("p c w -> p (c w)"),
+                    in_=bt[n][:].rearrange("p c w -> p (c w)"),
+                )
 
         def one_pass(n, m, c):
             nc.tensor.matmul_mx(
@@ -177,39 +209,54 @@ def tile_relukanlayer_kernel(tc, x, base_weight, spline_weight, spline_scale, gr
                     for c in range(PASSES):
                         one_pass(n, m, c)
 
-        def evac(n):
+        def on_vector(u, m):
+            return u == last_unit and m in V_EVAC_M
+
+        def evac(n, who):
             for m in range(MT):
                 for u, g0, gn, col in tile_segs[n]:
+                    if on_vector(u, m) != (who == "V"):
+                        continue
                     i0, r = units[u]
                     if (u, m) not in osb:
                         osb[(u, m)] = outp.tile([P, r, G], F32, name="osb%d_%d" % (u, m), tag="osb")
-                    nc.scalar.activation(
-                        out=osb[(u, m)][:, :, g0 : g0 + gn],
-                        in_=acc[(n, m)][:, col : col + gn * r].rearrange("p (g i) -> p i g", g=gn),
-                        func=ACT.Copy,
-                        scale=sc_f[:, m : m + 1],
-                    )
+                    src = acc[(n, m)][:, col : col + gn * r].rearrange("p (g i) -> p i g", g=gn)
+                    dst = osb[(u, m)][:, :, g0 : g0 + gn]
+                    if who == "V":
+                        nc.vector.tensor_scalar(out=dst, in0=src, scalar1=sc_f[:, m : m + 1], scalar2=None, op0=ALU.mult)
+                    else:
+                        nc.scalar.activation(out=dst, in_=src, func=ACT.Copy, scale=sc_f[:, m : m + 1])
                     if last_tile[u] == n:
                         nc.sync.dma_start(out=out[P * m : P * (m + 1), i0 : i0 + r, :], in_=osb[(u, m)][:])
 
         x_regroup("V", 0)
-        g_regroup("S", 0)
-        g_regroup("S", 1)
         x_regroup("S", 1)
-        basis(0)
-        quant(0)
+        g_regroup("S", 0, 0, OUT)
+        if G1_SPLIT:
+            g_regroup("S", 1, 0, OUT // 2)
+        else:
+            g_regroup("S", 1, 0, OUT)
+        x_regroup("S", 2)
+        basis(0, "all")
+        basis(1, "a")
+        quant(0, False)
+        if G1_SPLIT:
+            g_regroup("V", 1, OUT // 2, OUT)
         g_quant(0)
-        basis(1)
+        basis(1, "b")
+        basis(2, "a")
         g_quant(1)
         mm(0, True)
-        evac(0)
+        evac(0, "S")
         for s in range(1, NT):
+            quant(s, False)
             if s in V_XRG_BEFORE:
                 x_regroup("V", V_XRG_BEFORE[s])
             if s + 1 < NT:
-                basis(s + 1)
-            quant(s)
+                basis(s + 1, "b")
+            if s + 2 < NT:
+                basis(s + 2, "a")
             mm(s, False)
-            evac(s)
+            evac(s, "S")
             if s in S_XRG_AFTER:
                 x_regroup("S", S_XRG_AFTER[s])

@@ -24,12 +24,12 @@ BYTES = 2 * B * IN + 2 * B * OUT + 2 * OUT + 2 * G + 4 * OUT * IN * G
 
 UNITS = [64] * 8
 PIECES = [(0, 64), (64, 64), (128, 128), (256, 128), (384, 128)]
-S_XRG_AFTER = {3: 3, 8: 4}
+S_XRG_AFTER = {8: 4}
 V_XRG_BEFORE = {}
 V_EVAC_M = ()
 OSB_BUFS = 16
 LEAD_ELEMS = 1280
-G1_SPLIT = True
+S_XRG_HEAD = (2, 3)
 
 
 def tile_relukanlayer_kernel(tc, x, base_weight, spline_weight, spline_scale, grid, grad_out, out):
@@ -229,33 +229,25 @@ def tile_relukanlayer_kernel(tc, x, base_weight, spline_weight, spline_scale, gr
                     if last_tile[u] == n:
                         nc.sync.dma_start(out=out[P * m : P * (m + 1), i0 : i0 + r, :], in_=osb[(u, m)][:])
 
-        x_regroup("V", 0)
+        x_regroup("S", 0)
         x_regroup("S", 1)
         g_regroup("S", 0, 0, OUT)
-        if G1_SPLIT:
-            g_regroup("S", 1, 0, OUT // 2)
-        else:
-            g_regroup("S", 1, 0, OUT)
-        x_regroup("S", 2)
+        g_regroup("S", 1, 0, OUT)
+        for k in S_XRG_HEAD:
+            x_regroup("S", k)
         basis(0, "all")
-        basis(1, "a")
+        basis(1, "all")
         quant(0, False)
-        if G1_SPLIT:
-            g_regroup("V", 1, OUT // 2, OUT)
         g_quant(0)
-        basis(1, "b")
-        basis(2, "a")
         g_quant(1)
         mm(0, True)
         evac(0, "S")
         for s in range(1, NT):
-            quant(s, False)
             if s in V_XRG_BEFORE:
                 x_regroup("V", V_XRG_BEFORE[s])
             if s + 1 < NT:
-                basis(s + 1, "b")
-            if s + 2 < NT:
-                basis(s + 2, "a")
+                basis(s + 1, "all")
+            quant(s, False)
             mm(s, False)
             evac(s, "S")
             if s in S_XRG_AFTER:

@@ -28,6 +28,7 @@ S_XRG_AFTER = {8: 4}
 V_XRG_BEFORE = {}
 V_EVAC_M = ()
 OSB_BUFS = 16
+PADW = 48
 LEAD_ELEMS = 1280
 S_XRG_HEAD = (2, 3)
 
@@ -79,8 +80,8 @@ def tile_relukanlayer_kernel(tc, x, base_weight, spline_weight, spline_scale, gr
             xr_raw.append(keep.tile([P, PACK, IN - P], BF16, name="xr_raw%d" % c))
             g_raw.append(keep.tile([P, PACK, OUT], BF16, name="g_raw%d" % c))
             gg.append(keep.tile([P, PACK * OUT], BF16, name="gg%d" % c, align_bytes=64))
-            g_codes.append(keep.tile([P, OUT], U32, name="g_codes%d" % c, align_bytes=64))
-            g_scales.append(keep.tile([P, OUT], U8, name="g_scales%d" % c, align_bytes=64))
+            g_codes.append(keep.tile([P, PADW + OUT], U32, name="g_codes%d" % c, align_bytes=256))
+            g_scales.append(keep.tile([P, MT, 2 * P], U8, name="g_scales%d" % c, align_bytes=256))
         xg = []
         for k in range(len(PIECES)):
             xg.append(keep.tile([P, PASSES, PACK * PIECES[k][1]], BF16, name="xg%d" % k))
@@ -125,7 +126,12 @@ def tile_relukanlayer_kernel(tc, x, base_weight, spline_weight, spline_scale, gr
             regroup(eng, gg[c][:, PACK * lo : PACK * hi], g_raw[c][:, :, lo:hi])
 
         def g_quant(c):
-            nc.vector.quantize_mx(out=g_codes[c][:].bitcast(E5X4), scales=g_scales[c][:], in_=gg[c][:])
+            for m in range(MT):
+                nc.vector.quantize_mx(
+                    out=g_codes[c][:, PADW + P * m : PADW + P * (m + 1)].bitcast(E5X4),
+                    scales=g_scales[c][:, m, 0:P],
+                    in_=gg[c][:, PACK * P * m : PACK * P * (m + 1)],
+                )
 
         def piece_of(i0):
             for k in range(len(PIECES)):
@@ -172,8 +178,8 @@ def tile_relukanlayer_kernel(tc, x, base_weight, spline_weight, spline_scale, gr
                 )
 
         def quant(n, split):
-            codes = work.tile([P, PASSES, NCOL], U32, name="bc%d" % n, tag="bc", align_bytes=64)
-            scales = work.tile([P, PASSES, NCOL], U8, name="bs%d" % n, tag="bs", align_bytes=64)
+            codes = work.tile([P, PASSES, NCOL], U32, name="bc%d" % n, tag="bc", align_bytes=256)
+            scales = work.tile([P, PASSES, NCOL], U8, name="bs%d" % n, tag="bs", align_bytes=256)
             bc[n] = codes
             bs[n] = scales
             if split:
@@ -189,8 +195,8 @@ def tile_relukanlayer_kernel(tc, x, base_weight, spline_weight, spline_scale, gr
         def one_pass(n, m, c):
             nc.tensor.matmul_mx(
                 out=acc[(n, m)][:],
-                lhsT=g_codes[c][:, P * m : P * (m + 1)].bitcast(E5X4),
-                lhsT_scale=g_scales[c][:, P * m : P * (m + 1)],
+                lhsT=g_codes[c][:, PADW + P * m : PADW + P * (m + 1)].bitcast(E5X4),
+                lhsT_scale=g_scales[c][:, m, 0:P],
                 rhs=bc[n][:, c, :].bitcast(E4X4),
                 rhs_scale=bs[n][:, c, :],
                 start=(c == 0),

@@ -22,12 +22,12 @@ NT = IN * G // NCOL
 FLOPS = 2 * B * OUT * IN * G
 BYTES = 2 * B * IN + 2 * B * OUT + 2 * OUT + 2 * G + 4 * OUT * IN * G
 
-UNITS = [64] * 8
+UNITS = [32, 32] + [64] * 7
 PIECES = [(0, 64), (64, 64), (128, 128), (256, 128), (384, 128)]
 S_XRG_AFTER = {8: 4}
 V_XRG_BEFORE = {}
 V_EVAC_M = ()
-OSB_BUFS = 16
+OSB_BUFS = 18
 PADW = 48
 LEAD_ELEMS = 1280
 S_XRG_HEAD = (2, 3)

@@ -24,10 +24,11 @@ BYTES = 2 * B * IN + 2 * B * OUT + 2 * OUT + 2 * G + 4 * OUT * IN * G
 
 UNITS = [32, 32] + [64] * 7
 PIECES = [(0, 64), (64, 64), (128, 128), (256, 128), (384, 128)]
-S_XRG_AFTER = {8: 4}
-V_XRG_BEFORE = {}
-V_EVAC_M = ()
-OSB_BUFS = 18
+S_XRG_AFTER = {}
+V_XRG_BEFORE = {12: 4}
+V_EVAC = ((8, 2), (8, 3))
+WORK_BUFS = 4
+OSB_BUFS = 24
 PADW = 48
 LEAD_ELEMS = 1280
 S_XRG_HEAD = (2, 3)
@@ -64,7 +65,7 @@ def tile_relukanlayer_kernel(tc, x, base_weight, spline_weight, spline_scale, gr
 
     with ExitStack() as ctx:
         keep = ctx.enter_context(tc.tile_pool(name="keep", bufs=1))
-        work = ctx.enter_context(tc.tile_pool(name="work", bufs=3))
+        work = ctx.enter_context(tc.tile_pool(name="work", bufs=WORK_BUFS))
         outp = ctx.enter_context(tc.tile_pool(name="outp", bufs=OSB_BUFS))
         psum = ctx.enter_context(tc.psum_pool(name="psum", bufs=8))
         ctx.enter_context(tc.manual_schedule())
@@ -216,7 +217,7 @@ def tile_relukanlayer_kernel(tc, x, base_weight, spline_weight, spline_scale, gr
                         one_pass(n, m, c)
 
         def on_vector(u, m):
-            return u == last_unit and m in V_EVAC_M
+            return (u, m) in V_EVAC
 
         def evac(n, who):
             for m in range(MT):
@@ -254,7 +255,11 @@ def tile_relukanlayer_kernel(tc, x, base_weight, spline_weight, spline_scale, gr
             if s + 1 < NT:
                 basis(s + 1, "all")
             quant(s, False)
+            if s >= 2:
+                evac(s - 2, "V")
             mm(s, False)
             evac(s, "S")
             if s in S_XRG_AFTER:
                 x_regroup("S", S_XRG_AFTER[s])
+        evac(NT - 2, "V")
+        evac(NT - 1, "V")

@@ -24,11 +24,10 @@ BYTES = 2 * B * IN + 2 * B * OUT + 2 * OUT + 2 * G + 4 * OUT * IN * G
 
 UNITS = [32, 32] + [64] * 7
 PIECES = [(0, 64), (64, 64), (128, 128), (256, 128), (384, 128)]
-S_XRG_AFTER = {}
-V_XRG_BEFORE = {12: 4}
-V_EVAC = ((8, 2), (8, 3))
-WORK_BUFS = 4
-OSB_BUFS = 24
+S_XRG_AFTER = {8: 4}
+V_XRG_BEFORE = {}
+V_EVAC_M = ()
+OSB_BUFS = 18
 PADW = 48
 LEAD_ELEMS = 1280
 S_XRG_HEAD = (2, 3)
@@ -65,7 +64,7 @@ def tile_relukanlayer_kernel(tc, x, base_weight, spline_weight, spline_scale, gr
 
     with ExitStack() as ctx:
         keep = ctx.enter_context(tc.tile_pool(name="keep", bufs=1))
-        work = ctx.enter_context(tc.tile_pool(name="work", bufs=WORK_BUFS))
+        work = ctx.enter_context(tc.tile_pool(name="work", bufs=3))
         outp = ctx.enter_context(tc.tile_pool(name="outp", bufs=OSB_BUFS))
         psum = ctx.enter_context(tc.psum_pool(name="psum", bufs=8))
         ctx.enter_context(tc.manual_schedule())
@@ -217,7 +216,7 @@ def tile_relukanlayer_kernel(tc, x, base_weight, spline_weight, spline_scale, gr
                         one_pass(n, m, c)
 
         def on_vector(u, m):
-            return (u, m) in V_EVAC
+            return u == last_unit and m in V_EVAC_M
 
         def evac(n, who):
             for m in range(MT):
@@ -246,20 +245,17 @@ def tile_relukanlayer_kernel(tc, x, base_weight, spline_weight, spline_scale, gr
         basis(1, "all")
         quant(0, False)
         g_quant(0)
+        basis(2, "all")
         g_quant(1)
         mm(0, True)
         evac(0, "S")
         for s in range(1, NT):
             if s in V_XRG_BEFORE:
                 x_regroup("V", V_XRG_BEFORE[s])
-            if s + 1 < NT:
+            if 1 < s and s + 1 < NT:
                 basis(s + 1, "all")
             quant(s, False)
-            if s >= 2:
-                evac(s - 2, "V")
             mm(s, False)
             evac(s, "S")
             if s in S_XRG_AFTER:
                 x_regroup("S", S_XRG_AFTER[s])
-        evac(NT - 2, "V")
-        evac(NT - 1, "V")

from contextlib import ExitStack

import concourse.mybir as mybir

F32 = mybir.dt.float32
BF16 = mybir.dt.bfloat16
U32 = mybir.dt.uint32
U8 = mybir.dt.uint8
E4X4 = mybir.dt.float8_e4m3fn_x4
E5X4 = mybir.dt.float8_e5m2_x4
ALU = mybir.AluOpType
ACT = mybir.ActivationFunctionType

B, IN, OUT, G = 1024, 512, 512, 20
P = 128
PACK = 4
PASSES = B // (P * PACK)
MT = OUT // P
NCOL = 512
NT = IN * G // NCOL

FLOPS = 2 * B * OUT * IN * G
BYTES = 2 * B * IN + 2 * B * OUT + 2 * OUT + 2 * G + 4 * OUT * IN * G

UNITS = [32, 32] + [64] * 7
PIECES = [(0, 64), (64, 64), (128, 128), (256, 128), (384, 128)]
S_XRG_AFTER = {8: 4}
V_XRG_BEFORE = {}
V_EVAC_M = ()
OSB_BUFS = 18
PADW = 48
LEAD_ELEMS = 1280
S_XRG_HEAD = (2, 3)


def tile_relukanlayer_kernel(tc, x, base_weight, spline_weight, spline_scale, grid, grad_out, out):
    nc = tc.nc

    units = []
    i0 = 0
    for r in UNITS:
        units.append((i0, r))
        i0 += r
    assert i0 == IN
    tile_rows = []
    tile_segs = []
    for n in range(NT):
        tile_rows.append([])
        tile_segs.append([])
    last_tile = []
    for u in range(len(units)):
        i0, r = units[u]
        for g in range(G):
            col = G * i0 + g * r
            n = col // NCOL
            tile_rows[n].append((u, g, col % NCOL))
            segs = tile_segs[n]
            if len(segs) > 0 and segs[-1][0] == u:
                segs[-1] = (u, segs[-1][1], segs[-1][2] + 1, segs[-1][3])
            else:
                segs.append((u, g, 1, col % NCOL))
        last_tile.append(n)
    last_unit = len(units) - 1

    with ExitStack() as ctx:
        keep = ctx.enter_context(tc.tile_pool(name="keep", bufs=1))
        work = ctx.enter_context(tc.tile_pool(name="work", bufs=3))
        outp = ctx.enter_context(tc.tile_pool(name="outp", bufs=OSB_BUFS))
        psum = ctx.enter_context(tc.psum_pool(name="psum", bufs=8))
        ctx.enter_context(tc.manual_schedule())

        xa_raw = []
        xr_raw = []
        g_raw = []
        gg = []
        g_codes = []
        g_scales = []
        for c in range(PASSES):
            xa_raw.append(keep.tile([P, PACK, P], BF16, name="xa_raw%d" % c))
            xr_raw.append(keep.tile([P, PACK, IN - P], BF16, name="xr_raw%d" % c))
            g_raw.append(keep.tile([P, PACK, OUT], BF16, name="g_raw%d" % c))
            gg.append(keep.tile([P, PACK * OUT], BF16, name="gg%d" % c, align_bytes=64))
            g_codes.append(keep.tile([P, PADW + OUT], U32, name="g_codes%d" % c, align_bytes=256))
            g_scales.append(keep.tile([P, MT, 2 * P], U8, name="g_scales%d" % c, align_bytes=256))
        xg = []
        for k in range(len(PIECES)):
            xg.append(keep.tile([P, PASSES, PACK * PIECES[k][1]], BF16, name="xg%d" % k))
        grid_b = keep.tile([P, G], BF16, name="grid_b")
        grid_f = keep.tile([P, G], F32, name="grid_f")
        sc_b = keep.tile([P, MT], BF16, name="sc_b")
        sc_f = keep.tile([P, MT], F32, name="sc_f")

        x_v = x.rearrange("(c p j) i -> p c j i", c=PASSES, p=P, j=PACK)
        g_v = grad_out.rearrange("(c p j) o -> p c j o", c=PASSES, p=P, j=PACK)

        nc.sync.dma_start(out=grid_b[:], in_=grid.partition_broadcast(P))
        for c in range(PASSES):
            nc.sync.dma_start(out=xa_raw[c][:], in_=x_v[:, c, :, 0:P])
        for c in range(PASSES):
            nc.sync.dma_start(out=g_raw[c][:], in_=g_v[:, c, :, :])
        with nc.allow_non_contiguous_dma(reason="512 scales, one to a partition and m-tile"):
            nc.sync.dma_start(out=sc_b[:], in_=spline_scale.rearrange("(m p) a b -> p (m a b)", p=P))
        for c in range(PASSES):
            nc.sync.dma_start(out=xr_raw[c][:], in_=x_v[:, c, :, P:IN])

        nc.vector.tensor_copy(out=grid_f[:], in_=grid_b[:])
        nc.gpsimd.tensor_copy(out=sc_f[:], in_=sc_b[:])

        def regroup(eng, dst, src):
            d = dst.rearrange("p (q r j) -> p q j r", r=4, j=PACK)
            s = src.rearrange("p j (q r) -> p q j r", r=4)
            if eng == "V":
                nc.vector.tensor_copy(out=d, in_=s)
            else:
                nc.scalar.copy(out=d, in_=s)

        def x_regroup(eng, k):
            a, w = PIECES[k]
            for c in range(PASSES):
                if a < P:
                    regroup(eng, xg[k][:, c, :], xa_raw[c][:, :, a : a + w])
                else:
                    regroup(eng, xg[k][:, c, :], xr_raw[c][:, :, a - P : a - P + w])

        def g_regroup(eng, c, lo, hi):
            regroup(eng, gg[c][:, PACK * lo : PACK * hi], g_raw[c][:, :, lo:hi])

        def g_quant(c):
            for m in range(MT):
                nc.vector.quantize_mx(
                    out=g_codes[c][:, PADW + P * m : PADW + P * (m + 1)].bitcast(E5X4),
                    scales=g_scales[c][:, m, 0:P],
                    in_=gg[c][:, PACK * P * m : PACK * P * (m + 1)],
                )

        def piece_of(i0):
            for k in range(len(PIECES)):
                if PIECES[k][0] <= i0 < PIECES[k][0] + PIECES[k][1]:
                    return k
            return -1

        bt = {}
        bc = {}
        bs = {}
        acc = {}
        osb = {}

        def lead_rows(n):
            k = 0
            elems = 0
            for u, g, col in tile_rows[n]:
                if elems < LEAD_ELEMS:
                    elems += PASSES * PACK * units[u][1]
                    k += 1
            return k

        def basis(n, part):
            if n not in bt:
                bt[n] = work.tile([P, PASSES, PACK * NCOL], BF16, name="bt%d" % n, tag="bt", align_bytes=64)
            t = bt[n]
            k = lead_rows(n)
            rows = tile_rows[n]
            if part == "a":
                rows = tile_rows[n][:k]
            if part == "b":
                rows = tile_rows[n][k:]
            for u, g, col in rows:
                i0, r = units[u]
                k = piece_of(i0)
                off = i0 - PIECES[k][0]
                nc.vector.tensor_scalar(
                    out=t[:, :, PACK * col : PACK * (col + r)],
                    in0=xg[k][:, :, PACK * off : PACK * (off + r)],
                    scalar1=grid_f[:, g : g + 1],
                    scalar2=0.0,
                    op0=ALU.subtract,
                    op1=ALU.max,
                )

        def quant(n, split):
            codes = work.tile([P, PASSES, NCOL], U32, name="bc%d" % n, tag="bc", align_bytes=256)
            scales = work.tile([P, PASSES, NCOL], U8, name="bs%d" % n, tag="bs", align_bytes=256)
            bc[n] = codes
            bs[n] = scales
            if split:
                for c in range(PASSES):
                    nc.vector.quantize_mx(out=codes[:, c, :].bitcast(E4X4), scales=scales[:, c, :], in_=bt[n][:, c, :])
            else:
                nc.vector.quantize_mx(
                    out=codes[:].rearrange("p c w -> p (c w)").bitcast(E4X4),
                    scales=scales[:].rearrange("p c w -> p (c w)"),
                    in_=bt[n][:].rearrange("p c w -> p (c w)"),
                )

        def one_pass(n, m, c):
            nc.tensor.matmul_mx(
                out=acc[(n, m)][:],
                lhsT=g_codes[c][:, PADW + P * m : PADW + P * (m + 1)].bitcast(E5X4),
                lhsT_scale=g_scales[c][:, m, 0:P],
                rhs=bc[n][:, c, :].bitcast(E4X4),
                rhs_scale=bs[n][:, c, :],
                start=(c == 0),
                stop=(c == PASSES - 1),
            )

        def mm(n, c_major):
            for m in range(MT):
                acc[(n, m)] = psum.tile([P, NCOL], F32, name="acc%d_%d" % (n, m), tag="acc")
            if c_major:
                for c in range(PASSES):
                    for m in range(MT):
                        one_pass(n, m, c)
            else:
                for m in range(MT):
                    for c in range(PASSES):
                        one_pass(n, m, c)

        def on_vector(u, m):
            return u == last_unit and m in V_EVAC_M

        def evac(n, who):
            for m in range(MT):
                for u, g0, gn, col in tile_segs[n]:
                    if on_vector(u, m) != (who == "V"):
                        continue
                    i0, r = units[u]
                    if (u, m) not in osb:
                        osb[(u, m)] = outp.tile([P, r, G], F32, name="osb%d_%d" % (u, m), tag="osb")
                    src = acc[(n, m)][:, col : col + gn * r].rearrange("p (g i) -> p i g", g=gn)
                    dst = osb[(u, m)][:, :, g0 : g0 + gn]
                    if who == "V":
                        nc.vector.tensor_scalar(out=dst, in0=src, scalar1=sc_f[:, m : m + 1], scalar2=None, op0=ALU.mult)
                    else:
                        nc.scalar.activation(out=dst, in_=src, func=ACT.Copy, scale=sc_f[:, m : m + 1])
                    if last_tile[u] == n:
                        nc.sync.dma_start(out=out[P * m : P * (m + 1), i0 : i0 + r, :], in_=osb[(u, m)][:])

        x_regroup("S", 0)
        x_regroup("S", 1)
        g_regroup("S", 0, 0, OUT)
        g_regroup("S", 1, 0, OUT)
        for k in S_XRG_HEAD:
            x_regroup("S", k)
        basis(0, "all")
        basis(1, "all")
        quant(0, False)
        g_quant(0)
        basis(2, "all")
        g_quant(1)
        mm(0, True)
        evac(0, "S")
        for s in range(1, NT):
            if s in V_XRG_BEFORE:
                x_regroup("V", V_XRG_BEFORE[s])
            if 1 < s and s + 1 < NT:
                basis(s + 1, "all")
            quant(s, False)
            mm(s, False)
            evac(s, "S")
            if s in S_XRG_AFTER:
                x_regroup("S", S_XRG_AFTER[s])
